import numpy as np
import ml_dtypes


def mxq(x, axis, fmt="e4m3"):
    dtype, down = {"e4m3": (ml_dtypes.float8_e4m3fn, 7), "e5m2": (ml_dtypes.float8_e5m2, 14)}[fmt]
    v = np.moveaxis(np.asarray(x, np.float32).astype(ml_dtypes.bfloat16).astype(np.float64), axis, -1)
    blocks = v.reshape(v.shape[:-1] + (-1, 32))
    amax = np.abs(blocks).max(-1, keepdims=True)
    byte = np.maximum(np.where(amax > 0, np.frexp(amax)[1] - 1 + 127, 0) - down, 1)
    scale = np.exp2(byte - 127.0)
    codes = (blocks / scale).astype(np.float32).astype(dtype).astype(np.float64)
    return np.moveaxis((codes * scale).reshape(v.shape), -1, axis)


WIDE = False


def mx_kscale(k):
    if not WIDE:
        return np.ones(k)
    levels = np.array([10, -10, 5, -5, 0])
    a = np.random.permutation(np.resize(levels, k // 512 * 4)).reshape(k // 512, 4)
    idx = np.arange(k)
    return np.exp2(a[idx // 512, idx % 128 // 32])


BF16 = ml_dtypes.bfloat16


def bf(x):
    return np.asarray(x, np.float32).astype(BF16)


def f64(x):
    return np.asarray(x).astype(np.float64)


E2M1 = np.array([0.0, 0.5, 1.0, 1.5, 2.0, 3.0, 4.0, 6.0, -0.0, -0.5, -1.0, -1.5, -2.0, -3.0, -4.0, -6.0])


def pack_weight(w, fmt):
    k, n = w.shape
    w = f64(bf(w)).reshape(k // 32, 32, n)
    amax = np.abs(w).max(1)
    if fmt == "e4m3":
        byte = np.frexp(amax)[1] - 1 + 127 - 7
    else:
        mant, ex = np.frexp(amax / 6.0)
        byte = np.where(mant > 0.5, ex, ex - 1) + 127
    byte = np.clip(np.where(amax > 0, byte, 1), 1, 254)
    scaled = (w * np.exp2(127.0 - byte)[:, None, :]).reshape(k, n).astype(np.float32)
    by_word = np.ascontiguousarray(scaled.reshape(k // 512, 128, 4, n).transpose(0, 1, 3, 2))
    if fmt == "e4m3":
        words = by_word.astype(ml_dtypes.float8_e4m3fn).view(np.uint8)
    else:
        c = by_word.astype(ml_dtypes.float4_e2m1fn).view(np.uint8) & 0xF
        words = c[..., 0::2] | (c[..., 1::2] << 4)
    return np.ascontiguousarray(words), np.ascontiguousarray(byte.astype(np.uint8).reshape(k // 512, 16, n))


def unpack_weight(words, scales, fmt):
    g, p, n, _ = words.shape
    if fmt == "e4m3":
        vals = np.ascontiguousarray(words).view(ml_dtypes.float8_e4m3fn).astype(np.float64)
    else:
        nib = np.empty((g, p, n, 4), np.uint8)
        nib[..., 0::2] = words & 0xF
        nib[..., 1::2] = words >> 4
        vals = E2M1[nib]
    vals = vals * np.repeat(np.exp2(scales.astype(np.float64) - 127.0), 8, axis=1)[..., None]
    return vals.transpose(0, 1, 3, 2).reshape(g * 512, n)


B, S, D, P, N1, N2, N3 = 2, 512, 1024, 128, 3, 2, 3
H = N1 + N2 + N3
H1 = N2 + N3


def setup_inputs():
    s = mx_kscale(D)
    a = 1.0 / np.sqrt(D)
    x = bf(np.random.standard_normal((B, S, D)) * s)
    w_now = np.random.standard_normal((H, P, D)) * a / s
    w_back1 = np.random.standard_normal((N2 + N3, P, D)) * a / s
    w_back2 = np.random.standard_normal((N3, P, D)) * a / s
    bias = bf(np.random.standard_normal((H, P)) * 0.5)
    w_now_words, w_now_scales = pack_weight(w_now.swapaxes(1, 2).reshape(-1, P), "e4m3")
    w_back1_words, w_back1_scales = pack_weight(w_back1.swapaxes(1, 2).reshape(-1, P), "e4m3")
    w_back2_words, w_back2_scales = pack_weight(w_back2.swapaxes(1, 2).reshape(-1, P), "e4m3")
    return {"x": x,
            "w_now_words": w_now_words, "w_now_scales": w_now_scales,
            "w_back1_words": w_back1_words, "w_back1_scales": w_back1_scales,
            "w_back2_words": w_back2_words, "w_back2_scales": w_back2_scales,
            "bias": bias}


def reference(x, w_now_words, w_now_scales, w_back1_words, w_back1_scales, w_back2_words, w_back2_scales, bias):
    xq = mxq(f64(x), 2, "e4m3")
    w_now = unpack_weight(w_now_words, w_now_scales, "e4m3").reshape(H, D, P).swapaxes(1, 2)
    w_back1 = unpack_weight(w_back1_words, w_back1_scales, "e4m3").reshape(H1, D, P).swapaxes(1, 2)
    w_back2 = unpack_weight(w_back2_words, w_back2_scales, "e4m3").reshape(N3, D, P).swapaxes(1, 2)
    y = 0.0
    for j, w in enumerate((w_now, w_back1, w_back2)):
        z = xq @ w.reshape(-1, D).T
        y = y + np.pad(z[:, :S - j], ((0, 0), (j, 0), (H * P - z.shape[-1], 0)))
    return y.reshape(B, S, H, P).transpose(0, 2, 1, 3) + f64(bias)[None, :, None, :]

@@ -1,0 +1,210 @@
+from contextlib import ExitStack
+
+import concourse.mybir as mybir
+from concourse.masks import make_identity
+
+F32 = mybir.dt.float32
+BF16 = mybir.dt.bfloat16
+I32 = mybir.dt.int32
+U32 = mybir.dt.uint32
+U8 = mybir.dt.uint8
+FP8X4 = mybir.dt.float8_e4m3fn_x4
+
+P = 128
+SEQS = 2
+SEQ_LEN = 512
+K = 1024
+K_PASS = 512
+PASSES = K // K_PASS
+HEADS = 8
+HEAD_DIM = 128
+TAPS = 3
+FIRST_HEAD = (0, 3, 5)
+TILES = SEQS * SEQ_LEN // P
+WORDS = K // 2
+BANK = 512
+HEAD_GROUPS = ((0, 2), (2, 1), (3, 2), (5, 2), (7, 1))
+LOAD_GROUPS = ((0, 3), (3, 2), (5, 3))
+
+FLOPS = 2 * SEQS * SEQ_LEN * K * HEAD_DIM * (8 + 5 + 3)
+
+
+def taps_of(head):
+    return len([first for first in FIRST_HEAD if head >= first])
+
+
+def tile_multiheadhomogeneousattention_pa_e_kernel(
+    tc,
+    x,
+    w_now_words,
+    w_now_scales,
+    w_back1_words,
+    w_back1_scales,
+    w_back2_words,
+    w_back2_scales,
+    bias,
+    out,
+):
+    nc = tc.nc
+    words_in = (w_now_words, w_back1_words, w_back2_words)
+    scales_in = (w_now_scales, w_back1_scales, w_back2_scales)
+
+    x_view = x.rearrange("n (m i) k -> m n (i k)", i=TILES)
+    out_view = out.rearrange("n h (m i) d -> h m n (i d)", i=TILES)
+
+    with ExitStack() as ctx:
+        keep = ctx.enter_context(tc.tile_pool(name="keep", bufs=1))
+        stage = ctx.enter_context(tc.tile_pool(name="stage", bufs=3))
+        psum = ctx.enter_context(tc.psum_pool(name="psum", bufs=8))
+
+        x_sb = keep.tile([P, TILES * K], BF16)
+        x_codes = keep.tile([P, TILES + 2, PASSES, P], U32, align_bytes=64)
+        x_planes = keep.tile([P, TILES + 2, PASSES, P], U8, align_bytes=64)
+        w_codes = []
+        w_planes = []
+        w_rows = []
+        for tap in range(TAPS):
+            heads = HEADS - FIRST_HEAD[tap]
+            w_codes.append(
+                keep.tile([P, PASSES, heads, HEAD_DIM], U32, align_bytes=64, name="w_codes%d" % tap)
+            )
+            w_planes.append(
+                keep.tile([P, PASSES, heads, HEAD_DIM], U8, align_bytes=64, name="w_planes%d" % tap)
+            )
+            w_rows.append(keep.tile([P, heads, PASSES, HEAD_DIM // 4], I32, name="w_rows%d" % tap))
+        bias_rows = keep.tile([P, HEADS * HEAD_DIM], BF16)
+        bias_all = keep.tile([P, HEADS, HEAD_DIM], F32)
+        ones = keep.tile([P, P], BF16)
+        ident = keep.tile([P, P], F32)
+        y = keep.tile([P, HEADS, TILES, HEAD_DIM], F32)
+
+        for tap in range(TAPS):
+            nc.vector.memset(w_rows[tap][:], 0)
+        make_identity(nc, ident[:])
+        nc.gpsimd.memset(bias_rows[:], 0.0)
+        nc.gpsimd.memset(ones[:], 1.0)
+
+        def load_x(first_tile, tiles):
+            cols = slice(first_tile * K, (first_tile + tiles) * K)
+            nc.sync.dma_start(out=x_sb[:, cols], in_=x_view[:, :, cols])
+
+        def load_scales(tap):
+            rows = scales_in[tap].bitcast(I32).rearrange("g (a r) w -> r a g w", r=4)
+            for r in range(4):
+                nc.sync.dma_start(
+                    out=w_rows[tap][r:P:32].rearrange("q h c w -> q (h c) w"), in_=rows[r]
+                )
+
+        def load_words(tap, first_head, heads):
+            src = (
+                words_in[tap]
+                .rearrange("g p n t -> g p (n t)")
+                .bitcast(I32)
+                .rearrange("(h c) p w -> c p h w", c=PASSES)
+            )
+            h0 = first_head - FIRST_HEAD[tap]
+            for c in range(PASSES):
+                nc.sync.dma_start(
+                    out=w_codes[tap][:, c, h0 : h0 + heads, :].bitcast(I32),
+                    in_=src[c][:, h0 : h0 + heads, :],
+                )
+
+        load_x(0, 2)
+        load_scales(0)
+        load_x(2, 2)
+        load_x(4, 2)
+        load_x(6, 2)
+        nc.sync.dma_start(out=bias_rows[0:1, :], in_=bias.rearrange("(o h) d -> o (h d)", o=1))
+        for first_head, heads in LOAD_GROUPS:
+            for tap in range(1, taps_of(first_head)):
+                if first_head == FIRST_HEAD[tap]:
+                    load_scales(tap)
+            for tap in range(taps_of(first_head)):
+                load_words(tap, first_head, heads)
+
+        for tap in range(TAPS):
+            nc.vector.tensor_copy(
+                out=w_planes[tap][:].bitcast(I32),
+                in_=w_rows[tap][:].rearrange("p h c w -> p c h w"),
+            )
+
+        x_words = x_sb[:].bitcast(F32)
+        for i in range(TILES):
+            turned = psum.tile([P, PASSES, 2, P], F32, tag="bank")
+            for c in range(PASSES):
+                for u in range(2):
+                    first = i * WORDS + c * (K_PASS // 2) + u
+                    nc.tensor.transpose(
+                        turned[:, c, u, :],
+                        x_words[:, first : first + K_PASS // 2 - u : 2],
+                        ident[:],
+                    )
+            grouped = stage.tile([P, PASSES, P, 4], BF16, align_bytes=64)
+            nc.scalar.copy(
+                out=grouped[:].bitcast(F32), in_=turned[:].rearrange("p c u m -> p c m u")
+            )
+            nc.vector.quantize_mx(
+                out=x_codes[:, i + 2].rearrange("p c m -> p (c m)").bitcast(FP8X4),
+                scales=x_planes[:, i + 2].rearrange("p c m -> p (c m)"),
+                in_=grouped[:].rearrange("p c m t -> p (c m t)"),
+            )
+            if i >= TILES - 2:
+                moved = stage.tile([P, PASSES, P, 4], BF16, align_bytes=64)
+                nc.vector.memset(moved[:, :, 0:SEQS, :], 0.0)
+                nc.vector.tensor_copy(out=moved[:, :, SEQS:P, :], in_=grouped[:, :, 0 : P - SEQS, :])
+                nc.vector.quantize_mx(
+                    out=x_codes[:, i + 2 - TILES].rearrange("p c m -> p (c m)").bitcast(FP8X4),
+                    scales=x_planes[:, i + 2 - TILES].rearrange("p c m -> p (c m)"),
+                    in_=moved[:].rearrange("p c m t -> p (c m t)"),
+                )
+
+        for half in range(HEADS * HEAD_DIM // BANK):
+            spread = psum.tile([P, BANK], F32, tag="bank")
+            nc.tensor.matmul(
+                out=spread[:],
+                lhsT=ones[:],
+                rhs=bias_rows[:, half * BANK : (half + 1) * BANK],
+                start=True,
+                stop=True,
+            )
+            nc.scalar.copy(
+                out=bias_all[:].rearrange("p h d -> p (h d)")[:, half * BANK : (half + 1) * BANK],
+                in_=spread[:],
+            )
+
+        for first_head, heads in HEAD_GROUPS:
+            taps = taps_of(first_head)
+            per_bank = BANK // (heads * HEAD_DIM)
+            for i0 in range(0, TILES, per_bank):
+                sums = psum.tile([P, per_bank, heads, HEAD_DIM], F32, tag="bank")
+                for i in range(i0, i0 + per_bank):
+                    for tap in range(taps):
+                        h0 = first_head - FIRST_HEAD[tap]
+                        for c in range(PASSES):
+                            nc.tensor.matmul_mx(
+                                out=sums[:, i - i0].rearrange("p h d -> p (h d)"),
+                                lhsT=x_codes[:, i - tap + 2, c, :].bitcast(FP8X4),
+                                lhsT_scale=x_planes[:, i - tap + 2, c, :],
+                                rhs=w_codes[tap][:, c, h0 : h0 + heads, :]
+                                .rearrange("p h d -> p (h d)")
+                                .bitcast(FP8X4),
+                                rhs_scale=w_planes[tap][:, c, h0 : h0 + heads, :].rearrange(
+                                    "p h d -> p (h d)"
+                                ),
+                                start=(tap == 0 and c == 0),
+                                stop=(tap == taps - 1 and c == PASSES - 1),
+                            )
+                nc.vector.tensor_tensor(
+                    out=y[:, first_head : first_head + heads, i0 : i0 + per_bank, :].rearrange(
+                        "p h i d -> p i h d"
+                    ),
+                    in0=sums[:],
+                    in1=bias_all[:, first_head : first_head + heads, :]
+                    .unsqueeze(1)
+                    .to_broadcast([P, per_bank, heads, HEAD_DIM]),
+                    op=mybir.AluOpType.add,
+                )
+            for head in range(first_head, first_head + heads):
+                nc.sync.dma_start(
+                    out=out_view[head], in_=y[:, head].rearrange("p i d -> p (i d)")
+                )

@@ -81,18 +81,19 @@ def tile_multiheadhomogeneousattention_pa_e_kernel(
         for tap in range(TAPS):
             nc.vector.memset(w_rows[tap][:], 0)
         make_identity(nc, ident[:])
-        nc.gpsimd.memset(bias_rows[:], 0.0)
-        nc.gpsimd.memset(ones[:], 1.0)
+        nc.vector.memset(bias_rows[:], 0.0)
+        nc.vector.memset(ones[:], 1.0)
 
         def load_x(first_tile, tiles):
             cols = slice(first_tile * K, (first_tile + tiles) * K)
             nc.sync.dma_start(out=x_sb[:, cols], in_=x_view[:, :, cols])
 
         def load_scales(tap):
-            rows = scales_in[tap].bitcast(I32).rearrange("g (a r) w -> r a g w", r=4)
+            rows = scales_in[tap].bitcast(F32).rearrange("g (a r) w -> r a g w", r=4)
             for r in range(4):
-                nc.sync.dma_start(
-                    out=w_rows[tap][r:P:32].rearrange("q h c w -> q (h c) w"), in_=rows[r]
+                nc.gpsimd.dma_start(
+                    out=w_rows[tap][r:P:32].bitcast(F32).rearrange("q h c w -> q (h c) w"),
+                    in_=rows[r],
                 )
 
         def load_words(tap, first_head, heads):
@@ -109,16 +110,14 @@ def tile_multiheadhomogeneousattention_pa_e_kernel(
                     in_=src[c][:, h0 : h0 + heads, :],
                 )
 
+        for tap in range(TAPS):
+            load_scales(tap)
         load_x(0, 2)
-        load_scales(0)
         load_x(2, 2)
         load_x(4, 2)
         load_x(6, 2)
         nc.sync.dma_start(out=bias_rows[0:1, :], in_=bias.rearrange("(o h) d -> o (h d)", o=1))
         for first_head, heads in LOAD_GROUPS:
-            for tap in range(1, taps_of(first_head)):
-                if first_head == FIRST_HEAD[tap]:
-                    load_scales(tap)
             for tap in range(taps_of(first_head)):
                 load_words(tap, first_head, heads)
 

@@ -23,8 +23,10 @@ FIRST_HEAD = (0, 3, 5)
 TILES = SEQS * SEQ_LEN // P
 WORDS = K // 2
 BANK = 512
+BANK_TILES = 2
+STORE_TILES = 4
 HEAD_GROUPS = ((0, 2), (2, 1), (3, 2), (5, 2), (7, 1))
-LOAD_GROUPS = ((0, 3), (3, 2), (5, 3))
+LOAD_GROUPS = ((0, 2), (2, 1), (3, 2), (5, 3))
 
 FLOPS = 2 * SEQS * SEQ_LEN * K * HEAD_DIM * (8 + 5 + 3)
 
@@ -81,19 +83,18 @@ def tile_multiheadhomogeneousattention_pa_e_kernel(
         for tap in range(TAPS):
             nc.vector.memset(w_rows[tap][:], 0)
         make_identity(nc, ident[:])
-        nc.vector.memset(bias_rows[:], 0.0)
-        nc.vector.memset(ones[:], 1.0)
+        nc.gpsimd.memset(bias_rows[:], 0.0)
+        nc.gpsimd.memset(ones[:], 1.0)
 
         def load_x(first_tile, tiles):
             cols = slice(first_tile * K, (first_tile + tiles) * K)
             nc.sync.dma_start(out=x_sb[:, cols], in_=x_view[:, :, cols])
 
         def load_scales(tap):
-            rows = scales_in[tap].bitcast(F32).rearrange("g (a r) w -> r a g w", r=4)
+            rows = scales_in[tap].bitcast(I32).rearrange("g (a r) w -> r a g w", r=4)
             for r in range(4):
-                nc.gpsimd.dma_start(
-                    out=w_rows[tap][r:P:32].bitcast(F32).rearrange("q h c w -> q (h c) w"),
-                    in_=rows[r],
+                nc.sync.dma_start(
+                    out=w_rows[tap][r:P:32].rearrange("q h c w -> q (h c) w"), in_=rows[r]
                 )
 
         def load_words(tap, first_head, heads):
@@ -110,22 +111,18 @@ def tile_multiheadhomogeneousattention_pa_e_kernel(
                     in_=src[c][:, h0 : h0 + heads, :],
                 )
 
-        for tap in range(TAPS):
-            load_scales(tap)
         load_x(0, 2)
+        load_scales(0)
         load_x(2, 2)
         load_x(4, 2)
         load_x(6, 2)
         nc.sync.dma_start(out=bias_rows[0:1, :], in_=bias.rearrange("(o h) d -> o (h d)", o=1))
         for first_head, heads in LOAD_GROUPS:
+            for tap in range(1, taps_of(first_head)):
+                if first_head == FIRST_HEAD[tap]:
+                    load_scales(tap)
             for tap in range(taps_of(first_head)):
                 load_words(tap, first_head, heads)
-
-        for tap in range(TAPS):
-            nc.vector.tensor_copy(
-                out=w_planes[tap][:].bitcast(I32),
-                in_=w_rows[tap][:].rearrange("p h c w -> p c h w"),
-            )
 
         x_words = x_sb[:].bitcast(F32)
         for i in range(TILES):
@@ -173,37 +170,47 @@ def tile_multiheadhomogeneousattention_pa_e_kernel(
 
         for first_head, heads in HEAD_GROUPS:
             taps = taps_of(first_head)
-            per_bank = BANK // (heads * HEAD_DIM)
-            for i0 in range(0, TILES, per_bank):
-                sums = psum.tile([P, per_bank, heads, HEAD_DIM], F32, tag="bank")
-                for i in range(i0, i0 + per_bank):
-                    for tap in range(taps):
-                        h0 = first_head - FIRST_HEAD[tap]
-                        for c in range(PASSES):
-                            nc.tensor.matmul_mx(
-                                out=sums[:, i - i0].rearrange("p h d -> p (h d)"),
-                                lhsT=x_codes[:, i - tap + 2, c, :].bitcast(FP8X4),
-                                lhsT_scale=x_planes[:, i - tap + 2, c, :],
-                                rhs=w_codes[tap][:, c, h0 : h0 + heads, :]
-                                .rearrange("p h d -> p (h d)")
-                                .bitcast(FP8X4),
-                                rhs_scale=w_planes[tap][:, c, h0 : h0 + heads, :].rearrange(
-                                    "p h d -> p (h d)"
-                                ),
-                                start=(tap == 0 and c == 0),
-                                stop=(tap == taps - 1 and c == PASSES - 1),
-                            )
-                nc.vector.tensor_tensor(
-                    out=y[:, first_head : first_head + heads, i0 : i0 + per_bank, :].rearrange(
-                        "p h i d -> p i h d"
-                    ),
-                    in0=sums[:],
-                    in1=bias_all[:, first_head : first_head + heads, :]
-                    .unsqueeze(1)
-                    .to_broadcast([P, per_bank, heads, HEAD_DIM]),
-                    op=mybir.AluOpType.add,
-                )
-            for head in range(first_head, first_head + heads):
-                nc.sync.dma_start(
-                    out=out_view[head], in_=y[:, head].rearrange("p i d -> p (i d)")
-                )
+            for tap in range(taps):
+                if first_head == FIRST_HEAD[tap]:
+                    nc.vector.tensor_copy(
+                        out=w_planes[tap][:].bitcast(I32),
+                        in_=w_rows[tap][:].rearrange("p h c w -> p c h w"),
+                    )
+            for s0 in range(0, TILES, STORE_TILES):
+                for i0 in range(s0, s0 + STORE_TILES, BANK_TILES):
+                    bank = psum.tile([P, BANK], F32, tag="bank")
+                    sums = bank[:, 0 : BANK_TILES * heads * HEAD_DIM].rearrange(
+                        "p (i h d) -> p i h d", i=BANK_TILES, h=heads
+                    )
+                    for i in range(i0, i0 + BANK_TILES):
+                        for tap in range(taps):
+                            h0 = first_head - FIRST_HEAD[tap]
+                            for c in range(PASSES):
+                                nc.tensor.matmul_mx(
+                                    out=sums[:, i - i0].rearrange("p h d -> p (h d)"),
+                                    lhsT=x_codes[:, i - tap + 2, c, :].bitcast(FP8X4),
+                                    lhsT_scale=x_planes[:, i - tap + 2, c, :],
+                                    rhs=w_codes[tap][:, c, h0 : h0 + heads, :]
+                                    .rearrange("p h d -> p (h d)")
+                                    .bitcast(FP8X4),
+                                    rhs_scale=w_planes[tap][:, c, h0 : h0 + heads, :].rearrange(
+                                        "p h d -> p (h d)"
+                                    ),
+                                    start=(tap == 0 and c == 0),
+                                    stop=(tap == taps - 1 and c == PASSES - 1),
+                                )
+                    nc.vector.tensor_tensor(
+                        out=y[:, first_head : first_head + heads, i0 : i0 + BANK_TILES, :].rearrange(
+                            "p h i d -> p i h d"
+                        ),
+                        in0=sums,
+                        in1=bias_all[:, first_head : first_head + heads, :]
+                        .unsqueeze(1)
+                        .to_broadcast([P, BANK_TILES, heads, HEAD_DIM]),
+                        op=mybir.AluOpType.add,
+                    )
+                for head in range(first_head, first_head + heads):
+                    nc.sync.dma_start(
+                        out=out_view[head][:, :, s0 * HEAD_DIM : (s0 + STORE_TILES) * HEAD_DIM],
+                        in_=y[:, head, s0 : s0 + STORE_TILES, :].rearrange("p i d -> p (i d)"),
+                    )

@@ -23,10 +23,8 @@ FIRST_HEAD = (0, 3, 5)
 TILES = SEQS * SEQ_LEN // P
 WORDS = K // 2
 BANK = 512
-BANK_TILES = 2
 STORE_TILES = 4
-HEAD_GROUPS = ((0, 2), (2, 1), (3, 2), (5, 2), (7, 1))
-LOAD_GROUPS = ((0, 2), (2, 1), (3, 2), (5, 3))
+X_CHUNKS = ((0, 1), (1, 1), (2, 2), (4, 2), (6, 2))
 
 FLOPS = 2 * SEQS * SEQ_LEN * K * HEAD_DIM * (8 + 5 + 3)
 
@@ -56,10 +54,18 @@ def tile_multiheadhomogeneousattention_pa_e_kernel(
 
     with ExitStack() as ctx:
         keep = ctx.enter_context(tc.tile_pool(name="keep", bufs=1))
-        stage = ctx.enter_context(tc.tile_pool(name="stage", bufs=3))
-        psum = ctx.enter_context(tc.psum_pool(name="psum", bufs=8))
+        stage = ctx.enter_context(tc.tile_pool(name="stage", bufs=4))
+        psum = ctx.enter_context(tc.psum_pool(name="psum", bufs=7))
+        spare = ctx.enter_context(tc.psum_pool(name="spare", bufs=1))
+        ctx.enter_context(tc.manual_schedule())
 
-        x_sb = keep.tile([P, TILES * K], BF16)
+        x_words = {}
+        x_chunks = []
+        for first_tile, tiles in X_CHUNKS:
+            chunk = keep.tile([P, tiles * K], BF16, name="x_chunk%d" % first_tile)
+            x_chunks.append(chunk)
+            for i in range(tiles):
+                x_words[first_tile + i] = chunk[:, i * K : (i + 1) * K].bitcast(F32)
         x_codes = keep.tile([P, TILES + 2, PASSES, P], U32, align_bytes=64)
         x_planes = keep.tile([P, TILES + 2, PASSES, P], U8, align_bytes=64)
         w_codes = []
@@ -74,21 +80,28 @@ def tile_multiheadhomogeneousattention_pa_e_kernel(
                 keep.tile([P, PASSES, heads, HEAD_DIM], U8, align_bytes=64, name="w_planes%d" % tap)
             )
             w_rows.append(keep.tile([P, heads, PASSES, HEAD_DIM // 4], I32, name="w_rows%d" % tap))
-        bias_rows = keep.tile([P, HEADS * HEAD_DIM], BF16)
-        bias_all = keep.tile([P, HEADS, HEAD_DIM], F32)
-        ones = keep.tile([P, P], BF16)
+        bias_all = keep.tile([P, HEADS, HEAD_DIM], BF16)
         ident = keep.tile([P, P], F32)
-        y = keep.tile([P, HEADS, TILES, HEAD_DIM], F32)
+        filler = keep.tile([P, BANK], BF16)
+        unread = spare.tile([P, BANK], F32)
 
+        nc.gpsimd.memset(filler[:], 0.0)
+        make_identity(nc, ident[:])
         for tap in range(TAPS):
             nc.vector.memset(w_rows[tap][:], 0)
-        make_identity(nc, ident[:])
-        nc.gpsimd.memset(bias_rows[:], 0.0)
-        nc.gpsimd.memset(ones[:], 1.0)
+        nc.vector.memset(x_codes[:, 0:2, :, 0:SEQS].bitcast(I32), 0)
+        nc.vector.memset(
+            x_planes[:, 0:2]
+            .rearrange("p s c m -> p (s c m)")
+            .bitcast(I32)
+            .rearrange("p (r w) -> p r w", w=P // 4)[:, :, 0:1],
+            0,
+        )
 
-        def load_x(first_tile, tiles):
+        def load_x(number):
+            first_tile, tiles = X_CHUNKS[number]
             cols = slice(first_tile * K, (first_tile + tiles) * K)
-            nc.sync.dma_start(out=x_sb[:, cols], in_=x_view[:, :, cols])
+            nc.sync.dma_start(out=x_chunks[number][:], in_=x_view[:, :, cols])
 
         def load_scales(tap):
             rows = scales_in[tap].bitcast(I32).rearrange("g (a r) w -> r a g w", r=4)
@@ -111,106 +124,157 @@ def tile_multiheadhomogeneousattention_pa_e_kernel(
                     in_=src[c][:, h0 : h0 + heads, :],
                 )
 
-        load_x(0, 2)
+        load_x(0)
+        load_x(1)
+        load_x(2)
         load_scales(0)
-        load_x(2, 2)
-        load_x(4, 2)
-        load_x(6, 2)
-        nc.sync.dma_start(out=bias_rows[0:1, :], in_=bias.rearrange("(o h) d -> o (h d)", o=1))
-        for first_head, heads in LOAD_GROUPS:
-            for tap in range(1, taps_of(first_head)):
-                if first_head == FIRST_HEAD[tap]:
-                    load_scales(tap)
-            for tap in range(taps_of(first_head)):
-                load_words(tap, first_head, heads)
+        load_words(0, 0, 2)
+        load_x(3)
+        nc.sync.dma_start(
+            out=bias_all[:].rearrange("p h d -> p (h d)"),
+            in_=bias.rearrange("h d -> (h d)").partition_broadcast(P),
+        )
+        load_words(0, 2, 1)
+        load_x(4)
+        load_scales(1)
+        load_words(0, 3, 2)
+        load_words(1, 3, 2)
+        load_scales(2)
+        load_words(0, 5, 3)
+        load_words(1, 5, 3)
+        load_words(2, 5, 3)
 
-        x_words = x_sb[:].bitcast(F32)
-        for i in range(TILES):
+        def keep_busy(matmuls):
+            for number in range(matmuls):
+                nc.tensor.matmul(
+                    out=unread[:], lhsT=filler[:, 0:P], rhs=filler[:], start=True, stop=True
+                )
+
+        def turn(i):
             turned = psum.tile([P, PASSES, 2, P], F32, tag="bank")
             for c in range(PASSES):
                 for u in range(2):
-                    first = i * WORDS + c * (K_PASS // 2) + u
+                    first = c * (K_PASS // 2) + u
                     nc.tensor.transpose(
                         turned[:, c, u, :],
-                        x_words[:, first : first + K_PASS // 2 - u : 2],
+                        x_words[i][:, first : first + K_PASS // 2 - u : 2],
                         ident[:],
                     )
             grouped = stage.tile([P, PASSES, P, 4], BF16, align_bytes=64)
             nc.scalar.copy(
                 out=grouped[:].bitcast(F32), in_=turned[:].rearrange("p c u m -> p c m u")
             )
+            return grouped
+
+        def quantise(i, grouped):
             nc.vector.quantize_mx(
                 out=x_codes[:, i + 2].rearrange("p c m -> p (c m)").bitcast(FP8X4),
                 scales=x_planes[:, i + 2].rearrange("p c m -> p (c m)"),
                 in_=grouped[:].rearrange("p c m t -> p (c m t)"),
             )
-            if i >= TILES - 2:
-                moved = stage.tile([P, PASSES, P, 4], BF16, align_bytes=64)
-                nc.vector.memset(moved[:, :, 0:SEQS, :], 0.0)
-                nc.vector.tensor_copy(out=moved[:, :, SEQS:P, :], in_=grouped[:, :, 0 : P - SEQS, :])
-                nc.vector.quantize_mx(
-                    out=x_codes[:, i + 2 - TILES].rearrange("p c m -> p (c m)").bitcast(FP8X4),
-                    scales=x_planes[:, i + 2 - TILES].rearrange("p c m -> p (c m)"),
-                    in_=moved[:].rearrange("p c m t -> p (c m t)"),
+
+        def move_last_tiles():
+            nc.vector.tensor_copy(
+                out=x_codes[:, 0:2, :, SEQS:P].bitcast(I32),
+                in_=x_codes[:, TILES : TILES + 2, :, 0 : P - SEQS].bitcast(I32),
+            )
+            nc.vector.tensor_copy(
+                out=x_planes[:, 0:2, :, SEQS:P],
+                in_=x_planes[:, TILES : TILES + 2, :, 0 : P - SEQS],
+            )
+
+        def order_scales(tap):
+            nc.vector.tensor_copy(
+                out=w_planes[tap][:].bitcast(I32),
+                in_=w_rows[tap][:].rearrange("p h c w -> p c h w"),
+            )
+
+        y_tiles = {}
+
+        def multiply(first_head, heads, i0, tiles):
+            taps = taps_of(first_head)
+            s0 = i0 - i0 % STORE_TILES
+            if (first_head, s0) not in y_tiles:
+                y_tiles[(first_head, s0)] = keep.tile(
+                    [P, heads, STORE_TILES, HEAD_DIM], F32, name="y_%d_%d" % (first_head, s0)
+                )
+            y = y_tiles[(first_head, s0)]
+            bank = psum.tile([P, BANK], F32, tag="bank")
+            sums = bank[:, 0 : tiles * heads * HEAD_DIM].rearrange(
+                "p (i h d) -> p i h d", i=tiles, h=heads
+            )
+            for i in range(i0, i0 + tiles):
+                for tap in range(taps):
+                    h0 = first_head - FIRST_HEAD[tap]
+                    for c in range(PASSES):
+                        nc.tensor.matmul_mx(
+                            out=sums[:, i - i0].rearrange("p h d -> p (h d)"),
+                            lhsT=x_codes[:, i - tap + 2, c, :].bitcast(FP8X4),
+                            lhsT_scale=x_planes[:, i - tap + 2, c, :],
+                            rhs=w_codes[tap][:, c, h0 : h0 + heads, :]
+                            .rearrange("p h d -> p (h d)")
+                            .bitcast(FP8X4),
+                            rhs_scale=w_planes[tap][:, c, h0 : h0 + heads, :].rearrange(
+                                "p h d -> p (h d)"
+                            ),
+                            start=(tap == 0 and c == 0),
+                            stop=(tap == taps - 1 and c == PASSES - 1),
+                        )
+            nc.vector.tensor_tensor(
+                out=y[:, :, i0 - s0 : i0 - s0 + tiles, :].rearrange("p h i d -> p i h d"),
+                in0=sums,
+                in1=bias_all[:, first_head : first_head + heads, :]
+                .unsqueeze(1)
+                .to_broadcast([P, tiles, heads, HEAD_DIM]),
+                op=mybir.AluOpType.add,
+            )
+
+        def store(first_head, heads, i0, tiles=STORE_TILES):
+            s0 = i0 - i0 % STORE_TILES
+            y = y_tiles[(first_head, s0)]
+            for h in range(heads):
+                nc.sync.dma_start(
+                    out=out_view[first_head + h][:, :, i0 * HEAD_DIM : (i0 + tiles) * HEAD_DIM],
+                    in_=y[:, h, i0 - s0 : i0 - s0 + tiles, :].rearrange("p i d -> p (i d)"),
                 )
 
-        for half in range(HEADS * HEAD_DIM // BANK):
-            spread = psum.tile([P, BANK], F32, tag="bank")
-            nc.tensor.matmul(
-                out=spread[:],
-                lhsT=ones[:],
-                rhs=bias_rows[:, half * BANK : (half + 1) * BANK],
-                start=True,
-                stop=True,
-            )
-            nc.scalar.copy(
-                out=bias_all[:].rearrange("p h d -> p (h d)")[:, half * BANK : (half + 1) * BANK],
-                in_=spread[:],
-            )
+        keep_busy(5)
+        quantise(0, turn(0))
+        quantise(1, turn(1))
+        keep_busy(1)
+        order_scales(0)
+        quantise(2, turn(2))
+        quantise(3, turn(3))
+        keep_busy(1)
+        multiply(0, 2, 0, 2)
+        quantise(4, turn(4))
+        quantise(5, turn(5))
+        multiply(0, 2, 2, 2)
+        store(0, 2, 0)
+        multiply(2, 1, 0, 4)
+        store(2, 1, 0)
+        quantise(6, turn(6))
+        quantise(7, turn(7))
+        order_scales(1)
+        move_last_tiles()
+        multiply(0, 2, 4, 2)
+        multiply(0, 2, 6, 2)
+        store(0, 2, 4)
+        multiply(2, 1, 4, 4)
+        store(2, 1, 4)
+        order_scales(2)
 
-        for first_head, heads in HEAD_GROUPS:
-            taps = taps_of(first_head)
-            for tap in range(taps):
-                if first_head == FIRST_HEAD[tap]:
-                    nc.vector.tensor_copy(
-                        out=w_planes[tap][:].bitcast(I32),
-                        in_=w_rows[tap][:].rearrange("p h c w -> p c h w"),
-                    )
-            for s0 in range(0, TILES, STORE_TILES):
-                for i0 in range(s0, s0 + STORE_TILES, BANK_TILES):
-                    bank = psum.tile([P, BANK], F32, tag="bank")
-                    sums = bank[:, 0 : BANK_TILES * heads * HEAD_DIM].rearrange(
-                        "p (i h d) -> p i h d", i=BANK_TILES, h=heads
-                    )
-                    for i in range(i0, i0 + BANK_TILES):
-                        for tap in range(taps):
-                            h0 = first_head - FIRST_HEAD[tap]
-                            for c in range(PASSES):
-                                nc.tensor.matmul_mx(
-                                    out=sums[:, i - i0].rearrange("p h d -> p (h d)"),
-                                    lhsT=x_codes[:, i - tap + 2, c, :].bitcast(FP8X4),
-                                    lhsT_scale=x_planes[:, i - tap + 2, c, :],
-                                    rhs=w_codes[tap][:, c, h0 : h0 + heads, :]
-                                    .rearrange("p h d -> p (h d)")
-                                    .bitcast(FP8X4),
-                                    rhs_scale=w_planes[tap][:, c, h0 : h0 + heads, :].rearrange(
-                                        "p h d -> p (h d)"
-                                    ),
-                                    start=(tap == 0 and c == 0),
-                                    stop=(tap == taps - 1 and c == PASSES - 1),
-                                )
-                    nc.vector.tensor_tensor(
-                        out=y[:, first_head : first_head + heads, i0 : i0 + BANK_TILES, :].rearrange(
-                            "p h i d -> p i h d"
-                        ),
-                        in0=sums,
-                        in1=bias_all[:, first_head : first_head + heads, :]
-                        .unsqueeze(1)
-                        .to_broadcast([P, BANK_TILES, heads, HEAD_DIM]),
-                        op=mybir.AluOpType.add,
-                    )
-                for head in range(first_head, first_head + heads):
-                    nc.sync.dma_start(
-                        out=out_view[head][:, :, s0 * HEAD_DIM : (s0 + STORE_TILES) * HEAD_DIM],
-                        in_=y[:, head, s0 : s0 + STORE_TILES, :].rearrange("p i d -> p (i d)"),
-                    )
+        for first_head in (3, 5):
+            for i0 in range(0, TILES, 2):
+                multiply(first_head, 2, i0, 2)
+                if i0 % STORE_TILES == 2:
+                    store(first_head, 2, i0 - 2)
+        multiply(7, 1, 0, 2)
+        multiply(7, 1, 2, 2)
+        store(7, 1, 0)
+        multiply(7, 1, 4, 2)
+        store(7, 1, 4, 2)
+        multiply(7, 1, 6, 1)
+        store(7, 1, 6, 1)
+        multiply(7, 1, 7, 1)
+        store(7, 1, 7, 1)

@@ -80,13 +80,17 @@ def tile_multiheadhomogeneousattention_pa_e_kernel(
                 keep.tile([P, PASSES, heads, HEAD_DIM], U8, align_bytes=64, name="w_planes%d" % tap)
             )
             w_rows.append(keep.tile([P, heads, PASSES, HEAD_DIM // 4], I32, name="w_rows%d" % tap))
-        bias_all = keep.tile([P, HEADS, HEAD_DIM], BF16)
+        bias_rows = keep.tile([P, HEADS * HEAD_DIM], BF16)
+        bias_all = keep.tile([P, HEADS, HEAD_DIM], F32)
+        ones = keep.tile([P, P], BF16)
         ident = keep.tile([P, P], F32)
         filler = keep.tile([P, BANK], BF16)
         unread = spare.tile([P, BANK], F32)
 
-        nc.gpsimd.memset(filler[:], 0.0)
+        nc.gpsimd.memset(bias_rows[:], 0.0)
+        nc.gpsimd.memset(ones[:], 1.0)
         make_identity(nc, ident[:])
+        nc.vector.memset(filler[:], 0.0)
         for tap in range(TAPS):
             nc.vector.memset(w_rows[tap][:], 0)
         nc.vector.memset(x_codes[:, 0:2, :, 0:SEQS].bitcast(I32), 0)
@@ -125,15 +129,12 @@ def tile_multiheadhomogeneousattention_pa_e_kernel(
                 )
 
         load_x(0)
+        nc.sync.dma_start(out=bias_rows[0:1, :], in_=bias.rearrange("(o h) d -> o (h d)", o=1))
         load_x(1)
         load_x(2)
         load_scales(0)
         load_words(0, 0, 2)
         load_x(3)
-        nc.sync.dma_start(
-            out=bias_all[:].rearrange("p h d -> p (h d)"),
-            in_=bias.rearrange("h d -> (h d)").partition_broadcast(P),
-        )
         load_words(0, 2, 1)
         load_x(4)
         load_scales(1)
@@ -148,6 +149,23 @@ def tile_multiheadhomogeneousattention_pa_e_kernel(
             for number in range(matmuls):
                 nc.tensor.matmul(
                     out=unread[:], lhsT=filler[:, 0:P], rhs=filler[:], start=True, stop=True
+                )
+
+        def spread_bias():
+            for half in range(HEADS * HEAD_DIM // BANK):
+                spread = psum.tile([P, BANK], F32, tag="bank")
+                nc.tensor.matmul(
+                    out=spread[:],
+                    lhsT=ones[:],
+                    rhs=bias_rows[:, half * BANK : (half + 1) * BANK],
+                    start=True,
+                    stop=True,
+                )
+                nc.scalar.copy(
+                    out=bias_all[:].rearrange("p h d -> p (h d)")[
+                        :, half * BANK : (half + 1) * BANK
+                    ],
+                    in_=spread[:],
                 )
 
         def turn(i):
@@ -238,14 +256,13 @@ def tile_multiheadhomogeneousattention_pa_e_kernel(
                     in_=y[:, h, i0 - s0 : i0 - s0 + tiles, :].rearrange("p i d -> p (i d)"),
                 )
 
-        keep_busy(5)
+        keep_busy(4)
         quantise(0, turn(0))
         quantise(1, turn(1))
-        keep_busy(1)
+        spread_bias()
         order_scales(0)
         quantise(2, turn(2))
         quantise(3, turn(3))
-        keep_busy(1)
         multiply(0, 2, 0, 2)
         quantise(4, turn(4))
         quantise(5, turn(5))

@@ -131,12 +131,12 @@ def tile_multiheadhomogeneousattention_pa_e_kernel(
         load_x(0)
         nc.sync.dma_start(out=bias_rows[0:1, :], in_=bias.rearrange("(o h) d -> o (h d)", o=1))
         load_x(1)
-        load_x(2)
         load_scales(0)
-        load_words(0, 0, 2)
+        load_x(2)
         load_x(3)
-        load_words(0, 2, 1)
         load_x(4)
+        load_words(0, 0, 2)
+        load_words(0, 2, 1)
         load_scales(1)
         load_words(0, 3, 2)
         load_words(1, 3, 2)
@@ -161,7 +161,7 @@ def tile_multiheadhomogeneousattention_pa_e_kernel(
                     start=True,
                     stop=True,
                 )
-                nc.scalar.copy(
+                nc.vector.tensor_copy(
                     out=bias_all[:].rearrange("p h d -> p (h d)")[
                         :, half * BANK : (half + 1) * BANK
                     ],
@@ -260,27 +260,23 @@ def tile_multiheadhomogeneousattention_pa_e_kernel(
         quantise(0, turn(0))
         quantise(1, turn(1))
         spread_bias()
-        order_scales(0)
+        keep_busy(1)
         quantise(2, turn(2))
         quantise(3, turn(3))
-        multiply(0, 2, 0, 2)
-        quantise(4, turn(4))
-        quantise(5, turn(5))
-        multiply(0, 2, 2, 2)
-        store(0, 2, 0)
-        multiply(2, 1, 0, 4)
-        store(2, 1, 0)
-        quantise(6, turn(6))
-        quantise(7, turn(7))
+        order_scales(0)
+        for i in range(4, TILES):
+            quantise(i, turn(i))
         order_scales(1)
         move_last_tiles()
-        multiply(0, 2, 4, 2)
-        multiply(0, 2, 6, 2)
-        store(0, 2, 4)
-        multiply(2, 1, 4, 4)
-        store(2, 1, 4)
         order_scales(2)
 
+        for i0 in range(0, TILES, 2):
+            multiply(0, 2, i0, 2)
+            if i0 % STORE_TILES == 2:
+                store(0, 2, i0 - 2)
+        for i0 in range(0, TILES, STORE_TILES):
+            multiply(2, 1, i0, STORE_TILES)
+            store(2, 1, i0)
         for first_head in (3, 5):
             for i0 in range(0, TILES, 2):
                 multiply(first_head, 2, i0, 2)

@@ -87,10 +87,10 @@ def tile_multiheadhomogeneousattention_pa_e_kernel(
         filler = keep.tile([P, BANK], BF16)
         unread = spare.tile([P, BANK], F32)
 
+        nc.gpsimd.memset(filler[:], 0.0)
         nc.gpsimd.memset(bias_rows[:], 0.0)
         nc.gpsimd.memset(ones[:], 1.0)
         make_identity(nc, ident[:])
-        nc.vector.memset(filler[:], 0.0)
         for tap in range(TAPS):
             nc.vector.memset(w_rows[tap][:], 0)
         nc.vector.memset(x_codes[:, 0:2, :, 0:SEQS].bitcast(I32), 0)
@@ -129,10 +129,10 @@ def tile_multiheadhomogeneousattention_pa_e_kernel(
                 )
 
         load_x(0)
-        nc.sync.dma_start(out=bias_rows[0:1, :], in_=bias.rearrange("(o h) d -> o (h d)", o=1))
         load_x(1)
         load_scales(0)
         load_x(2)
+        nc.sync.dma_start(out=bias_rows[0:1, :], in_=bias.rearrange("(o h) d -> o (h d)", o=1))
         load_x(3)
         load_x(4)
         load_words(0, 0, 2)
@@ -259,13 +259,17 @@ def tile_multiheadhomogeneousattention_pa_e_kernel(
         keep_busy(4)
         quantise(0, turn(0))
         quantise(1, turn(1))
-        spread_bias()
-        keep_busy(1)
+        keep_busy(2)
         quantise(2, turn(2))
         quantise(3, turn(3))
         order_scales(0)
-        for i in range(4, TILES):
-            quantise(i, turn(i))
+        spread_bias()
+        keep_busy(1)
+        quantise(4, turn(4))
+        quantise(5, turn(5))
+        keep_busy(1)
+        quantise(6, turn(6))
+        quantise(7, turn(7))
         order_scales(1)
         move_last_tiles()
         order_scales(2)

@@ -209,7 +209,7 @@ def tile_multiheadhomogeneousattention_pa_e_kernel(
 
         y_tiles = {}
 
-        def multiply(first_head, heads, i0, tiles):
+        def multiply(first_head, heads, i0, tiles, through_scalar=False):
             taps = taps_of(first_head)
             s0 = i0 - i0 % STORE_TILES
             if (first_head, s0) not in y_tiles:
@@ -238,9 +238,14 @@ def tile_multiheadhomogeneousattention_pa_e_kernel(
                             start=(tap == 0 and c == 0),
                             stop=(tap == taps - 1 and c == PASSES - 1),
                         )
+            target = y[:, :, i0 - s0 : i0 - s0 + tiles, :].rearrange("p h i d -> p i h d")
+            source = sums
+            if through_scalar:
+                nc.scalar.copy(out=target, in_=sums)
+                source = target
             nc.vector.tensor_tensor(
-                out=y[:, :, i0 - s0 : i0 - s0 + tiles, :].rearrange("p h i d -> p i h d"),
-                in0=sums,
+                out=target,
+                in0=source,
                 in1=bias_all[:, first_head : first_head + heads, :]
                 .unsqueeze(1)
                 .to_broadcast([P, tiles, heads, HEAD_DIM]),
@@ -275,18 +280,18 @@ def tile_multiheadhomogeneousattention_pa_e_kernel(
         order_scales(2)
 
         for i0 in range(0, TILES, 2):
-            multiply(0, 2, i0, 2)
+            multiply(0, 2, i0, 2, i0 % STORE_TILES == 0)
             if i0 % STORE_TILES == 2:
                 store(0, 2, i0 - 2)
         for i0 in range(0, TILES, STORE_TILES):
-            multiply(2, 1, i0, STORE_TILES)
+            multiply(2, 1, i0, STORE_TILES, i0 == 0)
             store(2, 1, i0)
         for first_head in (3, 5):
             for i0 in range(0, TILES, 2):
-                multiply(first_head, 2, i0, 2)
+                multiply(first_head, 2, i0, 2, i0 % STORE_TILES == 0)
                 if i0 % STORE_TILES == 2:
                     store(first_head, 2, i0 - 2)
-        multiply(7, 1, 0, 2)
+        multiply(7, 1, 0, 2, True)
         multiply(7, 1, 2, 2)
         store(7, 1, 0)
         multiply(7, 1, 4, 2)

@@ -24,6 +24,8 @@ TILES = SEQS * SEQ_LEN // P
 WORDS = K // 2
 BANK = 512
 STORE_TILES = 4
+HEAD_GROUPS = ((2, 1), (0, 2), (3, 2), (5, 2), (7, 1))
+SCALE_PARTS = ((0, 0, 3), (0, 3, 5), (1, 3, 5), (2, 5, 3))
 X_CHUNKS = ((0, 1), (1, 1), (2, 2), (4, 2), (6, 2))
 
 FLOPS = 2 * SEQS * SEQ_LEN * K * HEAD_DIM * (8 + 5 + 3)
@@ -68,18 +70,27 @@ def tile_multiheadhomogeneousattention_pa_e_kernel(
                 x_words[first_tile + i] = chunk[:, i * K : (i + 1) * K].bitcast(F32)
         x_codes = keep.tile([P, TILES + 2, PASSES, P], U32, align_bytes=64)
         x_planes = keep.tile([P, TILES + 2, PASSES, P], U8, align_bytes=64)
-        w_codes = []
-        w_planes = []
-        w_rows = []
-        for tap in range(TAPS):
-            heads = HEADS - FIRST_HEAD[tap]
-            w_codes.append(
-                keep.tile([P, PASSES, heads, HEAD_DIM], U32, align_bytes=64, name="w_codes%d" % tap)
+        w_codes = {}
+        for first_head, heads in HEAD_GROUPS:
+            for tap in range(taps_of(first_head)):
+                w_codes[(tap, first_head)] = keep.tile(
+                    [P, PASSES, heads, HEAD_DIM],
+                    U32,
+                    align_bytes=64,
+                    name="w_codes_%d_%d" % (tap, first_head),
+                )
+        w_rows = {}
+        w_planes = {}
+        for tap, first_head, heads in SCALE_PARTS:
+            w_rows[(tap, first_head)] = keep.tile(
+                [P, heads, PASSES, HEAD_DIM // 4], I32, name="w_rows_%d_%d" % (tap, first_head)
             )
-            w_planes.append(
-                keep.tile([P, PASSES, heads, HEAD_DIM], U8, align_bytes=64, name="w_planes%d" % tap)
+            w_planes[(tap, first_head)] = keep.tile(
+                [P, PASSES, heads, HEAD_DIM],
+                U8,
+                align_bytes=64,
+                name="w_planes_%d_%d" % (tap, first_head),
             )
-            w_rows.append(keep.tile([P, heads, PASSES, HEAD_DIM // 4], I32, name="w_rows%d" % tap))
         bias_rows = keep.tile([P, HEADS * HEAD_DIM], BF16)
         bias_all = keep.tile([P, HEADS, HEAD_DIM], F32)
         ones = keep.tile([P, P], BF16)
@@ -87,12 +98,12 @@ def tile_multiheadhomogeneousattention_pa_e_kernel(
         filler = keep.tile([P, BANK], BF16)
         unread = spare.tile([P, BANK], F32)
 
-        nc.gpsimd.memset(filler[:], 0.0)
         nc.gpsimd.memset(bias_rows[:], 0.0)
+        nc.vector.memset(filler[:], 0.0)
         nc.gpsimd.memset(ones[:], 1.0)
         make_identity(nc, ident[:])
-        for tap in range(TAPS):
-            nc.vector.memset(w_rows[tap][:], 0)
+        for tap, first_head, heads in SCALE_PARTS:
+            nc.vector.memset(w_rows[(tap, first_head)][:], 0)
         nc.vector.memset(x_codes[:, 0:2, :, 0:SEQS].bitcast(I32), 0)
         nc.vector.memset(
             x_planes[:, 0:2]
@@ -107,11 +118,13 @@ def tile_multiheadhomogeneousattention_pa_e_kernel(
             cols = slice(first_tile * K, (first_tile + tiles) * K)
             nc.sync.dma_start(out=x_chunks[number][:], in_=x_view[:, :, cols])
 
-        def load_scales(tap):
+        def load_scales(tap, first_head, heads):
             rows = scales_in[tap].bitcast(I32).rearrange("g (a r) w -> r a g w", r=4)
+            g0 = (first_head - FIRST_HEAD[tap]) * PASSES
             for r in range(4):
                 nc.sync.dma_start(
-                    out=w_rows[tap][r:P:32].rearrange("q h c w -> q (h c) w"), in_=rows[r]
+                    out=w_rows[(tap, first_head)][r:P:32].rearrange("q h c w -> q (h c) w"),
+                    in_=rows[r][:, g0 : g0 + heads * PASSES, :],
                 )
 
         def load_words(tap, first_head, heads):
@@ -119,31 +132,36 @@ def tile_multiheadhomogeneousattention_pa_e_kernel(
                 words_in[tap]
                 .rearrange("g p n t -> g p (n t)")
                 .bitcast(I32)
-                .rearrange("(h c) p w -> c p h w", c=PASSES)
+                .rearrange("(h c) p w -> p c h w", c=PASSES)
             )
             h0 = first_head - FIRST_HEAD[tap]
-            for c in range(PASSES):
-                nc.sync.dma_start(
-                    out=w_codes[tap][:, c, h0 : h0 + heads, :].bitcast(I32),
-                    in_=src[c][:, h0 : h0 + heads, :],
-                )
+            dst = w_codes[(tap, first_head)][:].bitcast(I32)
+            if heads == 1:
+                nc.sync.dma_start(out=dst[:, :, 0, :], in_=src[:, :, h0, :])
+            else:
+                for c in range(PASSES):
+                    nc.sync.dma_start(out=dst[:, c], in_=src[:, c, h0 : h0 + heads, :])
 
         load_x(0)
         load_x(1)
-        load_scales(0)
-        load_x(2)
         nc.sync.dma_start(out=bias_rows[0:1, :], in_=bias.rearrange("(o h) d -> o (h d)", o=1))
+        load_x(2)
         load_x(3)
         load_x(4)
-        load_words(0, 0, 2)
+        load_scales(0, 0, 3)
         load_words(0, 2, 1)
-        load_scales(1)
+        load_words(0, 0, 2)
+        load_scales(0, 3, 5)
         load_words(0, 3, 2)
+        load_scales(1, 3, 5)
         load_words(1, 3, 2)
-        load_scales(2)
-        load_words(0, 5, 3)
-        load_words(1, 5, 3)
-        load_words(2, 5, 3)
+        load_scales(2, 5, 3)
+        load_words(0, 5, 2)
+        load_words(1, 5, 2)
+        load_words(2, 5, 2)
+        load_words(0, 7, 1)
+        load_words(1, 7, 1)
+        load_words(2, 7, 1)
 
         def keep_busy(matmuls):
             for number in range(matmuls):
@@ -201,11 +219,19 @@ def tile_multiheadhomogeneousattention_pa_e_kernel(
                 in_=x_planes[:, TILES : TILES + 2, :, 0 : P - SEQS],
             )
 
-        def order_scales(tap):
+        def order_scales(tap, first_head):
             nc.vector.tensor_copy(
-                out=w_planes[tap][:].bitcast(I32),
-                in_=w_rows[tap][:].rearrange("p h c w -> p c h w"),
+                out=w_planes[(tap, first_head)][:].bitcast(I32),
+                in_=w_rows[(tap, first_head)][:].rearrange("p h c w -> p c h w"),
             )
+
+        def scale_bytes(tap, c, first_head, heads):
+            for part_tap, part_head, part_heads in SCALE_PARTS:
+                if part_tap == tap and part_head <= first_head < part_head + part_heads:
+                    h0 = first_head - part_head
+                    return w_planes[(tap, part_head)][:, c, h0 : h0 + heads, :].rearrange(
+                        "p h d -> p (h d)"
+                    )
 
         y_tiles = {}
 
@@ -223,18 +249,15 @@ def tile_multiheadhomogeneousattention_pa_e_kernel(
             )
             for i in range(i0, i0 + tiles):
                 for tap in range(taps):
-                    h0 = first_head - FIRST_HEAD[tap]
                     for c in range(PASSES):
                         nc.tensor.matmul_mx(
                             out=sums[:, i - i0].rearrange("p h d -> p (h d)"),
                             lhsT=x_codes[:, i - tap + 2, c, :].bitcast(FP8X4),
                             lhsT_scale=x_planes[:, i - tap + 2, c, :],
-                            rhs=w_codes[tap][:, c, h0 : h0 + heads, :]
+                            rhs=w_codes[(tap, first_head)][:, c]
                             .rearrange("p h d -> p (h d)")
                             .bitcast(FP8X4),
-                            rhs_scale=w_planes[tap][:, c, h0 : h0 + heads, :].rearrange(
-                                "p h d -> p (h d)"
-                            ),
+                            rhs_scale=scale_bytes(tap, c, first_head, heads),
                             start=(tap == 0 and c == 0),
                             stop=(tap == taps - 1 and c == PASSES - 1),
                         )
@@ -264,33 +287,35 @@ def tile_multiheadhomogeneousattention_pa_e_kernel(
         keep_busy(4)
         quantise(0, turn(0))
         quantise(1, turn(1))
-        keep_busy(2)
+        spread_bias()
         quantise(2, turn(2))
         quantise(3, turn(3))
-        order_scales(0)
-        spread_bias()
         keep_busy(1)
         quantise(4, turn(4))
+        order_scales(0, 0)
         quantise(5, turn(5))
         keep_busy(1)
         quantise(6, turn(6))
         quantise(7, turn(7))
-        order_scales(1)
         move_last_tiles()
-        order_scales(2)
 
-        for i0 in range(0, TILES, 2):
-            multiply(0, 2, i0, 2, i0 % STORE_TILES == 0)
-            if i0 % STORE_TILES == 2:
-                store(0, 2, i0 - 2)
         for i0 in range(0, TILES, STORE_TILES):
             multiply(2, 1, i0, STORE_TILES, i0 == 0)
             store(2, 1, i0)
+            multiply(0, 2, i0, 2, True)
+            if i0 == 0:
+                order_scales(0, 3)
+            multiply(0, 2, i0 + 2, 2)
+            if i0 == 0:
+                order_scales(1, 3)
+            store(0, 2, i0)
         for first_head in (3, 5):
             for i0 in range(0, TILES, 2):
                 multiply(first_head, 2, i0, 2, i0 % STORE_TILES == 0)
                 if i0 % STORE_TILES == 2:
                     store(first_head, 2, i0 - 2)
+                if first_head == 3 and i0 == 2:
+                    order_scales(2, 5)
         multiply(7, 1, 0, 2, True)
         multiply(7, 1, 2, 2)
         store(7, 1, 0)

@@ -179,7 +179,8 @@ def tile_multiheadhomogeneousattention_pa_e_kernel(
                     start=True,
                     stop=True,
                 )
-                nc.vector.tensor_copy(
+                copy = nc.scalar.copy if half else nc.vector.tensor_copy
+                copy(
                     out=bias_all[:].rearrange("p h d -> p (h d)")[
                         :, half * BANK : (half + 1) * BANK
                     ],
@@ -302,12 +303,12 @@ def tile_multiheadhomogeneousattention_pa_e_kernel(
         for i0 in range(0, TILES, STORE_TILES):
             multiply(2, 1, i0, STORE_TILES, i0 == 0)
             store(2, 1, i0)
-            multiply(0, 2, i0, 2, True)
             if i0 == 0:
                 order_scales(0, 3)
-            multiply(0, 2, i0 + 2, 2)
+            multiply(0, 2, i0, 2, True)
             if i0 == 0:
                 order_scales(1, 3)
+            multiply(0, 2, i0 + 2, 2)
             store(0, 2, i0)
         for first_head in (3, 5):
             for i0 in range(0, TILES, 2):

@@ -25,7 +25,7 @@ WORDS = K // 2
 BANK = 512
 STORE_TILES = 4
 HEAD_GROUPS = ((2, 1), (0, 2), (3, 2), (5, 2), (7, 1))
-SCALE_PARTS = ((0, 0, 3), (0, 3, 5), (1, 3, 5), (2, 5, 3))
+SCALE_PARTS = ((0, 0, 5), (1, 3, 5), (0, 5, 3), (2, 5, 3))
 X_CHUNKS = ((0, 1), (1, 1), (2, 2), (4, 2), (6, 2))
 
 FLOPS = 2 * SEQS * SEQ_LEN * K * HEAD_DIM * (8 + 5 + 3)
@@ -148,15 +148,15 @@ def tile_multiheadhomogeneousattention_pa_e_kernel(
         load_x(2)
         load_x(3)
         load_x(4)
-        load_scales(0, 0, 3)
+        load_scales(0, 0, 5)
         load_words(0, 2, 1)
         load_words(0, 0, 2)
-        load_scales(0, 3, 5)
         load_words(0, 3, 2)
         load_scales(1, 3, 5)
         load_words(1, 3, 2)
-        load_scales(2, 5, 3)
+        load_scales(0, 5, 3)
         load_words(0, 5, 2)
+        load_scales(2, 5, 3)
         load_words(1, 5, 2)
         load_words(2, 5, 2)
         load_words(0, 7, 1)
@@ -303,8 +303,6 @@ def tile_multiheadhomogeneousattention_pa_e_kernel(
         for i0 in range(0, TILES, STORE_TILES):
             multiply(2, 1, i0, STORE_TILES, i0 == 0)
             store(2, 1, i0)
-            if i0 == 0:
-                order_scales(0, 3)
             multiply(0, 2, i0, 2, True)
             if i0 == 0:
                 order_scales(1, 3)
@@ -316,6 +314,7 @@ def tile_multiheadhomogeneousattention_pa_e_kernel(
                 if i0 % STORE_TILES == 2:
                     store(first_head, 2, i0 - 2)
                 if first_head == 3 and i0 == 2:
+                    order_scales(0, 5)
                     order_scales(2, 5)
         multiply(7, 1, 0, 2, True)
         multiply(7, 1, 2, 2)

@@ -98,10 +98,10 @@ def tile_multiheadhomogeneousattention_pa_e_kernel(
         filler = keep.tile([P, BANK], BF16)
         unread = spare.tile([P, BANK], F32)
 
-        nc.gpsimd.memset(bias_rows[:], 0.0)
-        nc.vector.memset(filler[:], 0.0)
-        nc.gpsimd.memset(ones[:], 1.0)
+        nc.gpsimd.memset(filler[:].bitcast(F32), 0.0)
         make_identity(nc, ident[:])
+        nc.gpsimd.memset(ones[:], 1.0)
+        nc.vector.memset(bias_rows[:].bitcast(F32), 0.0)
         for tap, first_head, heads in SCALE_PARTS:
             nc.vector.memset(w_rows[(tap, first_head)][:], 0)
         nc.vector.memset(x_codes[:, 0:2, :, 0:SEQS].bitcast(I32), 0)

@@ -99,9 +99,9 @@ def tile_multiheadhomogeneousattention_pa_e_kernel(
         unread = spare.tile([P, BANK], F32)
 
         nc.gpsimd.memset(filler[:].bitcast(F32), 0.0)
+        nc.gpsimd.memset(bias_rows[:].bitcast(F32), 0.0)
         make_identity(nc, ident[:])
         nc.gpsimd.memset(ones[:], 1.0)
-        nc.vector.memset(bias_rows[:].bitcast(F32), 0.0)
         for tap, first_head, heads in SCALE_PARTS:
             nc.vector.memset(w_rows[(tap, first_head)][:], 0)
         nc.vector.memset(x_codes[:, 0:2, :, 0:SEQS].bitcast(I32), 0)

@@ -163,10 +163,14 @@ def tile_multiheadhomogeneousattention_pa_e_kernel(
         load_words(1, 7, 1)
         load_words(2, 7, 1)
 
-        def keep_busy(matmuls):
+        def keep_busy(matmuls, cols=BANK):
             for number in range(matmuls):
                 nc.tensor.matmul(
-                    out=unread[:], lhsT=filler[:, 0:P], rhs=filler[:], start=True, stop=True
+                    out=unread[:, 0:cols],
+                    lhsT=filler[:, 0:P],
+                    rhs=filler[:, 0:cols],
+                    start=True,
+                    stop=True,
                 )
 
         def spread_bias():
@@ -291,11 +295,11 @@ def tile_multiheadhomogeneousattention_pa_e_kernel(
         spread_bias()
         quantise(2, turn(2))
         quantise(3, turn(3))
-        keep_busy(1)
+        keep_busy(1, BANK // 2)
         quantise(4, turn(4))
         order_scales(0, 0)
         quantise(5, turn(5))
-        keep_busy(1)
+        keep_busy(1, BANK // 2)
         quantise(6, turn(6))
         quantise(7, turn(7))
         move_last_tiles()

from contextlib import ExitStack

import concourse.mybir as mybir
from concourse.masks import make_identity

F32 = mybir.dt.float32
BF16 = mybir.dt.bfloat16
I32 = mybir.dt.int32
U32 = mybir.dt.uint32
U8 = mybir.dt.uint8
FP8X4 = mybir.dt.float8_e4m3fn_x4

P = 128
SEQS = 2
SEQ_LEN = 512
K = 1024
K_PASS = 512
PASSES = K // K_PASS
HEADS = 8
HEAD_DIM = 128
TAPS = 3
FIRST_HEAD = (0, 3, 5)
TILES = SEQS * SEQ_LEN // P
WORDS = K // 2
BANK = 512
STORE_TILES = 4
HEAD_GROUPS = ((2, 1), (0, 2), (3, 2), (5, 2), (7, 1))
SCALE_PARTS = ((0, 0, 5), (1, 3, 5), (0, 5, 3), (2, 5, 3))
X_CHUNKS = ((0, 1), (1, 1), (2, 2), (4, 2), (6, 2))

FLOPS = 2 * SEQS * SEQ_LEN * K * HEAD_DIM * (8 + 5 + 3)


def taps_of(head):
    return len([first for first in FIRST_HEAD if head >= first])


def tile_multiheadhomogeneousattention_pa_e_kernel(
    tc,
    x,
    w_now_words,
    w_now_scales,
    w_back1_words,
    w_back1_scales,
    w_back2_words,
    w_back2_scales,
    bias,
    out,
):
    nc = tc.nc
    words_in = (w_now_words, w_back1_words, w_back2_words)
    scales_in = (w_now_scales, w_back1_scales, w_back2_scales)

    x_view = x.rearrange("n (m i) k -> m n (i k)", i=TILES)
    out_view = out.rearrange("n h (m i) d -> h m n (i d)", i=TILES)

    with ExitStack() as ctx:
        keep = ctx.enter_context(tc.tile_pool(name="keep", bufs=1))
        stage = ctx.enter_context(tc.tile_pool(name="stage", bufs=4))
        psum = ctx.enter_context(tc.psum_pool(name="psum", bufs=7))
        spare = ctx.enter_context(tc.psum_pool(name="spare", bufs=1))
        ctx.enter_context(tc.manual_schedule())

        x_words = {}
        x_chunks = []
        for first_tile, tiles in X_CHUNKS:
            chunk = keep.tile([P, tiles * K], BF16, name="x_chunk%d" % first_tile)
            x_chunks.append(chunk)
            for i in range(tiles):
                x_words[first_tile + i] = chunk[:, i * K : (i + 1) * K].bitcast(F32)
        x_codes = keep.tile([P, TILES + 2, PASSES, P], U32, align_bytes=64)
        x_planes = keep.tile([P, TILES + 2, PASSES, P], U8, align_bytes=64)
        w_codes = {}
        for first_head, heads in HEAD_GROUPS:
            for tap in range(taps_of(first_head)):
                w_codes[(tap, first_head)] = keep.tile(
                    [P, PASSES, heads, HEAD_DIM],
                    U32,
                    align_bytes=64,
                    name="w_codes_%d_%d" % (tap, first_head),
                )
        w_rows = {}
        w_planes = {}
        for tap, first_head, heads in SCALE_PARTS:
            w_rows[(tap, first_head)] = keep.tile(
                [P, heads, PASSES, HEAD_DIM // 4], I32, name="w_rows_%d_%d" % (tap, first_head)
            )
            w_planes[(tap, first_head)] = keep.tile(
                [P, PASSES, heads, HEAD_DIM],
                U8,
                align_bytes=64,
                name="w_planes_%d_%d" % (tap, first_head),
            )
        bias_rows = keep.tile([P, HEADS * HEAD_DIM], BF16)
        bias_all = keep.tile([P, HEADS, HEAD_DIM], F32)
        ones = keep.tile([P, P], BF16)
        ident = keep.tile([P, P], F32)
        filler = keep.tile([P, BANK], BF16)
        unread = spare.tile([P, BANK], F32)

        nc.gpsimd.memset(filler[:].bitcast(F32), 0.0)
        nc.gpsimd.memset(bias_rows[:].bitcast(F32), 0.0)
        make_identity(nc, ident[:])
        nc.gpsimd.memset(ones[:], 1.0)
        for tap, first_head, heads in SCALE_PARTS:
            nc.vector.memset(w_rows[(tap, first_head)][:], 0)
        nc.vector.memset(x_codes[:, 0:2, :, 0:SEQS].bitcast(I32), 0)
        nc.vector.memset(
            x_planes[:, 0:2]
            .rearrange("p s c m -> p (s c m)")
            .bitcast(I32)
            .rearrange("p (r w) -> p r w", w=P // 4)[:, :, 0:1],
            0,
        )

        def load_x(number):
            first_tile, tiles = X_CHUNKS[number]
            cols = slice(first_tile * K, (first_tile + tiles) * K)
            nc.sync.dma_start(out=x_chunks[number][:], in_=x_view[:, :, cols])

        def load_scales(tap, first_head, heads):
            rows = scales_in[tap].bitcast(I32).rearrange("g (a r) w -> r a g w", r=4)
            g0 = (first_head - FIRST_HEAD[tap]) * PASSES
            for r in range(4):
                nc.sync.dma_start(
                    out=w_rows[(tap, first_head)][r:P:32].rearrange("q h c w -> q (h c) w"),
                    in_=rows[r][:, g0 : g0 + heads * PASSES, :],
                )

        def load_words(tap, first_head, heads):
            src = (
                words_in[tap]
                .rearrange("g p n t -> g p (n t)")
                .bitcast(I32)
                .rearrange("(h c) p w -> p c h w", c=PASSES)
            )
            h0 = first_head - FIRST_HEAD[tap]
            dst = w_codes[(tap, first_head)][:].bitcast(I32)
            if heads == 1:
                nc.sync.dma_start(out=dst[:, :, 0, :], in_=src[:, :, h0, :])
            else:
                for c in range(PASSES):
                    nc.sync.dma_start(out=dst[:, c], in_=src[:, c, h0 : h0 + heads, :])

        load_x(0)
        load_x(1)
        nc.sync.dma_start(out=bias_rows[0:1, :], in_=bias.rearrange("(o h) d -> o (h d)", o=1))
        load_x(2)
        load_x(3)
        load_x(4)
        load_scales(0, 0, 5)
        load_words(0, 2, 1)
        load_words(0, 0, 2)
        load_words(0, 3, 2)
        load_scales(1, 3, 5)
        load_words(1, 3, 2)
        load_scales(0, 5, 3)
        load_words(0, 5, 2)
        load_scales(2, 5, 3)
        load_words(1, 5, 2)
        load_words(2, 5, 2)
        load_words(0, 7, 1)
        load_words(1, 7, 1)
        load_words(2, 7, 1)

        def keep_busy(matmuls, cols=BANK):
            for number in range(matmuls):
                nc.tensor.matmul(
                    out=unread[:, 0:cols],
                    lhsT=filler[:, 0:P],
                    rhs=filler[:, 0:cols],
                    start=True,
                    stop=True,
                )

        def spread_bias():
            for half in range(HEADS * HEAD_DIM // BANK):
                spread = psum.tile([P, BANK], F32, tag="bank")
                nc.tensor.matmul(
                    out=spread[:],
                    lhsT=ones[:],
                    rhs=bias_rows[:, half * BANK : (half + 1) * BANK],
                    start=True,
                    stop=True,
                )
                copy = nc.scalar.copy if half else nc.vector.tensor_copy
                copy(
                    out=bias_all[:].rearrange("p h d -> p (h d)")[
                        :, half * BANK : (half + 1) * BANK
                    ],
                    in_=spread[:],
                )

        def turn(i):
            turned = psum.tile([P, PASSES, 2, P], F32, tag="bank")
            for c in range(PASSES):
                for u in range(2):
                    first = c * (K_PASS // 2) + u
                    nc.tensor.transpose(
                        turned[:, c, u, :],
                        x_words[i][:, first : first + K_PASS // 2 - u : 2],
                        ident[:],
                    )
            grouped = stage.tile([P, PASSES, P, 4], BF16, align_bytes=64)
            nc.scalar.copy(
                out=grouped[:].bitcast(F32), in_=turned[:].rearrange("p c u m -> p c m u")
            )
            return grouped

        def quantise(i, grouped):
            nc.vector.quantize_mx(
                out=x_codes[:, i + 2].rearrange("p c m -> p (c m)").bitcast(FP8X4),
                scales=x_planes[:, i + 2].rearrange("p c m -> p (c m)"),
                in_=grouped[:].rearrange("p c m t -> p (c m t)"),
            )

        def move_last_tiles():
            nc.vector.tensor_copy(
                out=x_codes[:, 0:2, :, SEQS:P].bitcast(I32),
                in_=x_codes[:, TILES : TILES + 2, :, 0 : P - SEQS].bitcast(I32),
            )
            nc.vector.tensor_copy(
                out=x_planes[:, 0:2, :, SEQS:P],
                in_=x_planes[:, TILES : TILES + 2, :, 0 : P - SEQS],
            )

        def order_scales(tap, first_head):
            nc.vector.tensor_copy(
                out=w_planes[(tap, first_head)][:].bitcast(I32),
                in_=w_rows[(tap, first_head)][:].rearrange("p h c w -> p c h w"),
            )

        def scale_bytes(tap, c, first_head, heads):
            for part_tap, part_head, part_heads in SCALE_PARTS:
                if part_tap == tap and part_head <= first_head < part_head + part_heads:
                    h0 = first_head - part_head
                    return w_planes[(tap, part_head)][:, c, h0 : h0 + heads, :].rearrange(
                        "p h d -> p (h d)"
                    )

        y_tiles = {}

        def multiply(first_head, heads, i0, tiles, through_scalar=False):
            taps = taps_of(first_head)
            s0 = i0 - i0 % STORE_TILES
            if (first_head, s0) not in y_tiles:
                y_tiles[(first_head, s0)] = keep.tile(
                    [P, heads, STORE_TILES, HEAD_DIM], F32, name="y_%d_%d" % (first_head, s0)
                )
            y = y_tiles[(first_head, s0)]
            bank = psum.tile([P, BANK], F32, tag="bank")
            sums = bank[:, 0 : tiles * heads * HEAD_DIM].rearrange(
                "p (i h d) -> p i h d", i=tiles, h=heads
            )
            for i in range(i0, i0 + tiles):
                for tap in range(taps):
                    for c in range(PASSES):
                        nc.tensor.matmul_mx(
                            out=sums[:, i - i0].rearrange("p h d -> p (h d)"),
                            lhsT=x_codes[:, i - tap + 2, c, :].bitcast(FP8X4),
                            lhsT_scale=x_planes[:, i - tap + 2, c, :],
                            rhs=w_codes[(tap, first_head)][:, c]
                            .rearrange("p h d -> p (h d)")
                            .bitcast(FP8X4),
                            rhs_scale=scale_bytes(tap, c, first_head, heads),
                            start=(tap == 0 and c == 0),
                            stop=(tap == taps - 1 and c == PASSES - 1),
                        )
            target = y[:, :, i0 - s0 : i0 - s0 + tiles, :].rearrange("p h i d -> p i h d")
            source = sums
            if through_scalar:
                nc.scalar.copy(out=target, in_=sums)
                source = target
            nc.vector.tensor_tensor(
                out=target,
                in0=source,
                in1=bias_all[:, first_head : first_head + heads, :]
                .unsqueeze(1)
                .to_broadcast([P, tiles, heads, HEAD_DIM]),
                op=mybir.AluOpType.add,
            )

        def store(first_head, heads, i0, tiles=STORE_TILES):
            s0 = i0 - i0 % STORE_TILES
            y = y_tiles[(first_head, s0)]
            for h in range(heads):
                nc.sync.dma_start(
                    out=out_view[first_head + h][:, :, i0 * HEAD_DIM : (i0 + tiles) * HEAD_DIM],
                    in_=y[:, h, i0 - s0 : i0 - s0 + tiles, :].rearrange("p i d -> p (i d)"),
                )

        keep_busy(4)
        quantise(0, turn(0))
        quantise(1, turn(1))
        spread_bias()
        quantise(2, turn(2))
        quantise(3, turn(3))
        keep_busy(1, BANK // 2)
        quantise(4, turn(4))
        order_scales(0, 0)
        quantise(5, turn(5))
        keep_busy(1, BANK // 2)
        quantise(6, turn(6))
        quantise(7, turn(7))
        move_last_tiles()

        for i0 in range(0, TILES, STORE_TILES):
            multiply(2, 1, i0, STORE_TILES, i0 == 0)
            store(2, 1, i0)
            multiply(0, 2, i0, 2, True)
            if i0 == 0:
                order_scales(1, 3)
            multiply(0, 2, i0 + 2, 2)
            store(0, 2, i0)
        for first_head in (3, 5):
            for i0 in range(0, TILES, 2):
                multiply(first_head, 2, i0, 2, i0 % STORE_TILES == 0)
                if i0 % STORE_TILES == 2:
                    store(first_head, 2, i0 - 2)
                if first_head == 3 and i0 == 2:
                    order_scales(0, 5)
                    order_scales(2, 5)
        multiply(7, 1, 0, 2, True)
        multiply(7, 1, 2, 2)
        store(7, 1, 0)
        multiply(7, 1, 4, 2)
        store(7, 1, 4, 2)
        multiply(7, 1, 6, 1)
        store(7, 1, 6, 1)
        multiply(7, 1, 7, 1)
        store(7, 1, 7, 1)
